import numpy as np
import ml_dtypes


def mxq(x, axis, fmt="e4m3"):
    dtype, down = {"e4m3": (ml_dtypes.float8_e4m3fn, 7), "e5m2": (ml_dtypes.float8_e5m2, 14)}[fmt]
    v = np.moveaxis(np.asarray(x, np.float32).astype(ml_dtypes.bfloat16).astype(np.float64), axis, -1)
    blocks = v.reshape(v.shape[:-1] + (-1, 32))
    amax = np.abs(blocks).max(-1, keepdims=True)
    byte = np.maximum(np.where(amax > 0, np.frexp(amax)[1] - 1 + 127, 0) - down, 1)
    scale = np.exp2(byte - 127.0)
    codes = (blocks / scale).astype(np.float32).astype(dtype).astype(np.float64)
    return np.moveaxis((codes * scale).reshape(v.shape), -1, axis)


WIDE = False


def mx_kscale(k):
    if not WIDE:
        return np.ones(k)
    levels = np.array([10, -10, 5, -5, 0])
    a = np.random.permutation(np.resize(levels, k // 512 * 4)).reshape(k // 512, 4)
    idx = np.arange(k)
    return np.exp2(a[idx // 512, idx % 128 // 32])


BF16 = ml_dtypes.bfloat16


def bf(x):
    return np.asarray(x, np.float32).astype(BF16)


def f64(x):
    return np.asarray(x).astype(np.float64)


B, S, HID, NH, HD, RD, RATIO = 1, 2048, 1024, 8, 128, 64, 4
THETA = 10000.0
NW = S // RATIO
HALF = RD // 2


def rope_tables(positions):
    inv_freq = 1.0 / THETA ** (np.arange(HALF) / HALF)
    ang = positions[:, None] * inv_freq[None, :]
    return np.cos(ang), np.sin(ang)


def rope_interleaved(x, cos, sin):
    nope, rope = x[..., :-RD], x[..., -RD:]
    pr = rope.reshape(rope.shape[:-1] + (HALF, 2))
    a, b = pr[..., 0], pr[..., 1]
    new = np.stack([a * cos - b * sin, a * sin + b * cos], axis=-1).reshape(rope.shape)
    return np.concatenate([nope, new], axis=-1)


def remap(t, fill):
    cur = t[..., HD:]
    prev = np.concatenate([np.full((B, 1, RATIO, HD), fill), t[:, :-1, :, :HD]], axis=1)
    return np.concatenate([prev, cur], axis=2)


def pool_overlap(kv, gate, ape):
    kv_o = remap(kv.reshape(B, NW, RATIO, 2 * HD), 0.0)
    gate_o = remap(gate.reshape(B, NW, RATIO, 2 * HD) + ape, -np.inf)
    e = np.exp(gate_o - gate_o.max(axis=2, keepdims=True))
    w = e / e.sum(axis=2, keepdims=True)
    return (kv_o * w).sum(axis=2)


def setup_inputs():
    s = mx_kscale(HID)
    return {"hidden": bf(np.random.standard_normal((B, S, HID)) * s),
            "wkv": bf(np.random.standard_normal((HID, 2 * HD)) * 2.0 / np.sqrt(HID) / s[:, None]),
            "wgate": bf(np.random.standard_normal((HID, 2 * HD)) / np.sqrt(HID) / s[:, None]),
            "ape": bf(np.random.standard_normal((RATIO, 2 * HD)) * 0.5)}


def reference(hidden, wkv, wgate, ape):
    hq = mxq(f64(hidden), 2, "e4m3")
    kv = hq @ mxq(f64(wkv), 0, "e4m3")
    gate = hq @ mxq(f64(wgate), 0, "e4m3")
    pooled = pool_overlap(kv, gate, f64(ape))
    ck, sk = rope_tables(np.arange(NW) * RATIO)
    k_rot = rope_interleaved(pooled, ck, sk)
    return k_rot, pooled

@@ -1,0 +1,243 @@
+import math
+from contextlib import ExitStack
+
+import concourse.mybir as mybir
+from concourse.masks import make_identity
+
+F32 = mybir.dt.float32
+BF16 = mybir.dt.bfloat16
+I32 = mybir.dt.int32
+U32 = mybir.dt.uint32
+U8 = mybir.dt.uint8
+FP8X4 = mybir.dt.float8_e4m3fn_x4
+ALU = mybir.AluOpType
+ACT = mybir.ActivationFunctionType
+
+P = 128
+S, HID, HD, RD, RATIO = 2048, 1024, 128, 64, 4
+THETA = 10000.0
+HALF = RD // 2
+NOPE = HD - RD
+PACK = 4
+PASSES = HID // (P * PACK)
+CHUNKS = S // RATIO // P
+SLOTS = 2 * RATIO
+LO, HI = 0, 1
+ROUND = 1.5 * 2.0**23
+
+FLOPS = 2 * S * HID * 4 * HD
+
+
+def tile_deepseekv4attention_pa_kernel(tc, hidden, wkv, wgate, ape, out_0, out_1):
+    nc = tc.nc
+    hidden_chunks = hidden.flatten_outer_dims().rearrange("(i c r) k -> c i (r k)", c=CHUNKS, r=RATIO)
+    k_rot_chunks = out_0.flatten_outer_dims().rearrange("(i c) f -> c i f", c=CHUNKS)
+    pooled_chunks = out_1.flatten_outer_dims().rearrange("(i c) f -> c i f", c=CHUNKS)
+
+    with ExitStack() as ctx:
+        const = ctx.enter_context(tc.tile_pool(name="const", bufs=1))
+        weights = ctx.enter_context(tc.tile_pool(name="weights", bufs=2))
+        tokens = ctx.enter_context(tc.tile_pool(name="tokens", bufs=CHUNKS))
+        stage_in = ctx.enter_context(tc.tile_pool(name="stage_in", bufs=3))
+        soft = ctx.enter_context(tc.tile_pool(name="soft", bufs=2))
+        psum_flip = ctx.enter_context(tc.psum_pool(name="psum_flip", bufs=3))
+        psum_mx = ctx.enter_context(tc.psum_pool(name="psum_mx", bufs=1))
+        psum_sum = ctx.enter_context(tc.psum_pool(name="psum_sum", bufs=1))
+
+        def load_weight(w):
+            raw = weights.tile([P, PASSES, PACK, 2 * HD], BF16, name="w_raw")
+            nc.sync.dma_start(
+                out=raw[:].rearrange("p g (u e) c -> p (g u) (e c)", e=2),
+                in_=w.rearrange("(gu p e) c -> p gu (e c)", p=P, e=2),
+            )
+            return raw
+
+        def load_chunk(c):
+            raw = tokens.tile([P, RATIO * HID], BF16, name="x_raw")
+            for half in range(2):
+                cols = slice(half * 2 * HID, (half + 1) * 2 * HID)
+                nc.sync.dma_start(out=raw[:, cols], in_=hidden_chunks[c][:, cols])
+            return raw
+
+        ape_rows = const.tile([P, P], BF16)
+        nc.vector.memset(ape_rows[:], 0.0)
+        nc.scalar.dma_start(out=ape_rows[0:SLOTS, :], in_=ape.rearrange("r (h f) -> (r h) f", h=2))
+        wgate_raw = load_weight(wgate)
+        x_raw = [load_chunk(0), load_chunk(1)]
+        wkv_raw = load_weight(wkv)
+        x_raw.extend([load_chunk(2), load_chunk(3)])
+
+        ident = const.tile([P, P], F32)
+        make_identity(nc, ident[:])
+
+        position_int = const.tile([P, CHUNKS], I32)
+        nc.gpsimd.iota(position_int[:], pattern=[[RATIO, CHUNKS]], base=0, channel_multiplier=RATIO * CHUNKS)
+        position = const.tile([P, CHUNKS], F32)
+        nc.vector.tensor_copy(out=position[:], in_=position_int[:])
+        turns = const.tile([P, CHUNKS, HALF], F32)
+        for j in range(HALF):
+            nc.vector.tensor_single_scalar(
+                out=turns[:, :, j], in_=position[:], scalar=THETA ** (-j / HALF) / (2.0 * math.pi), op=ALU.mult
+            )
+        whole_turns = const.tile([P, CHUNKS, HALF], F32)
+        nc.vector.tensor_scalar(
+            out=whole_turns[:], in0=turns[:], scalar1=ROUND, scalar2=ROUND, op0=ALU.add, op1=ALU.subtract
+        )
+        phase = const.tile([P, 2, CHUNKS, HALF], F32)
+        nc.vector.tensor_tensor(out=phase[:, 0], in0=turns[:], in1=whole_turns[:], op=ALU.subtract)
+        nc.vector.scalar_tensor_tensor(
+            out=phase[:, 1], in0=phase[:, 0], scalar=-1.0, in1=phase[:, 0], op0=ALU.mult, op1=ALU.min
+        )
+        nc.vector.tensor_single_scalar(out=phase[:, 1], in_=phase[:, 1], scalar=0.25, op=ALU.add)
+        sin_cos = const.tile([P, 2, CHUNKS, HALF], F32)
+        nc.scalar.activation(out=sin_cos[:], in_=phase[:], func=ACT.Sin, scale=2.0 * math.pi)
+        neg_sin = const.tile([P, CHUNKS, HALF], F32)
+        nc.vector.tensor_single_scalar(out=neg_sin[:], in_=sin_cos[:, 0], scalar=-1.0, op=ALU.mult)
+
+        ape_rows_f32 = const.tile([P, P], F32)
+        nc.vector.tensor_copy(out=ape_rows_f32[:], in_=ape_rows[:])
+        ape_flip = psum_flip.tile([P, PASSES * 2, P], F32, tag="flip")
+        nc.tensor.transpose(ape_flip[:, 0, :], ape_rows_f32[:], ident[:])
+        ape_col = const.tile([P, SLOTS], F32)
+        nc.vector.tensor_copy(out=ape_col[:], in_=ape_flip[:, 0, 0:SLOTS])
+
+        def offset(r, half):
+            return ape_col[:, 2 * r + half : 2 * r + half + 1]
+
+        def quantise_weight(raw, copy):
+            grouped = weights.tile([P, PASSES, 2 * HD, PACK], BF16, align_bytes=64, name="w_grouped")
+            for g in range(PASSES):
+                copy(
+                    out=grouped[:, g].rearrange("p (c i) t -> p c t i", i=4),
+                    in_=raw[:, g].rearrange("p t (c i) -> p c t i", i=4),
+                )
+            codes = weights.tile([P, PASSES, 2 * HD], U32, align_bytes=64, name="w_codes")
+            scales = weights.tile([P, PASSES, 2 * HD], U8, align_bytes=64, name="w_scales")
+            nc.vector.quantize_mx(
+                out=codes[:].rearrange("p g c -> p (g c)").bitcast(FP8X4),
+                scales=scales[:].rearrange("p g c -> p (g c)"),
+                in_=grouped[:].rearrange("p g c t -> p (g c t)"),
+            )
+            return codes, scales
+
+        def quantise_chunk(raw):
+            words = raw[:].bitcast(F32)
+            codes = tokens.tile([P, PASSES, RATIO * P], U32, align_bytes=64, name="x_codes")
+            scales = tokens.tile([P, PASSES, RATIO * P], U8, align_bytes=64, name="x_scales")
+            for pair in range(RATIO // 2):
+                grouped = stage_in.tile([P, PASSES, 2, P * PACK], BF16, align_bytes=64, name="x_grouped")
+                grouped_words = grouped[:].bitcast(F32)
+                for r2 in range(2):
+                    first = (2 * pair + r2) * PASSES * 2
+                    flip = psum_flip.tile([P, PASSES * 2, P], F32, tag="flip")
+                    for q in range(PASSES * 2):
+                        nc.tensor.transpose(flip[:, q, :], words[:, (first + q) * P : (first + q + 1) * P], ident[:])
+                    nc.scalar.copy(
+                        out=grouped_words[:, :, r2, :].rearrange("p g (i u) -> p g i u", u=2),
+                        in_=flip[:].rearrange("p (g u) i -> p g i u", u=2),
+                    )
+                cols = slice(pair * 2 * P, (pair + 1) * 2 * P)
+                for g in range(PASSES):
+                    nc.vector.quantize_mx(
+                        out=codes[:, g, cols].bitcast(FP8X4),
+                        scales=scales[:, g, cols],
+                        in_=grouped[:, g].rearrange("p r x -> p (r x)"),
+                    )
+            return codes, scales
+
+        def project(w, half, x, tag):
+            w_codes, w_scales = w
+            x_codes, x_scales = x
+            features = slice(half * HD, (half + 1) * HD)
+            product = psum_mx.tile([P, RATIO, P], F32, tag=tag)
+            for g in range(PASSES):
+                nc.tensor.matmul_mx(
+                    out=product[:].rearrange("p r i -> p (r i)"),
+                    lhsT=w_codes[:, g, features].bitcast(FP8X4),
+                    lhsT_scale=w_scales[:, g, features],
+                    rhs=x_codes[:, g, :].bitcast(FP8X4),
+                    rhs_scale=x_scales[:, g, :],
+                    start=(g == 0),
+                    stop=(g == PASSES - 1),
+                )
+            return product
+
+        def pool_windows(c, gate, kv):
+            shift = 1 if c == 0 else 0
+            source = (slice(0, P - shift), slice(0, P))
+            window = (slice(shift, P), slice(0, P))
+            slots = (slice(0, RATIO), slice(RATIO, SLOTS))
+
+            top = [soft.tile([P, P], F32, name="top_lo"), soft.tile([P, P], F32, name="top_hi")]
+            for r in range(RATIO):
+                for half in (LO, HI):
+                    if r == 0:
+                        nc.vector.tensor_scalar(
+                            out=top[half][:, window[half]], in0=gate[half][:, r, source[half]],
+                            scalar1=offset(r, half), scalar2=None, op0=ALU.add,
+                        )
+                    else:
+                        nc.vector.scalar_tensor_tensor(
+                            out=top[half][:, window[half]], in0=gate[half][:, r, source[half]],
+                            scalar=offset(r, half), in1=top[half][:, window[half]], op0=ALU.add, op1=ALU.max,
+                        )
+            nc.vector.tensor_tensor(
+                out=top[HI][:, window[LO]], in0=top[HI][:, window[LO]], in1=top[LO][:, window[LO]], op=ALU.max
+            )
+
+            weight = soft.tile([P, SLOTS, P], F32)
+            weighted = soft.tile([P, SLOTS, P], F32)
+            if shift:
+                nc.vector.memset(weight[:, slots[LO], 0:shift], 0.0)
+                nc.vector.memset(weighted[:, slots[LO], 0:shift], 0.0)
+            for half in (LO, HI):
+                width = P - shift if half == LO else P
+                nc.vector.tensor_tensor(
+                    out=weight[:, slots[half], window[half]], in0=gate[half][:, :, source[half]],
+                    in1=top[HI][:, window[half]].unsqueeze(1).to_broadcast([P, RATIO, width]), op=ALU.subtract,
+                )
+                for r in range(RATIO):
+                    one = weight[:, half * RATIO + r, window[half]]
+                    nc.scalar.activation(out=one, in_=one, func=ACT.Exp, bias=offset(r, half), scale=1.0)
+            for half in (LO, HI):
+                nc.vector.tensor_tensor(
+                    out=weighted[:, slots[half], window[half]], in0=weight[:, slots[half], window[half]],
+                    in1=kv[half][:, :, source[half]], op=ALU.mult,
+                )
+
+            sums = psum_sum.tile([P, 2, P], F32)
+            for which, terms in enumerate((weight, weighted)):
+                for slot in range(SLOTS):
+                    nc.tensor.matmul(
+                        out=sums[:, which, :], lhsT=terms[:, slot, :], rhs=ident[:], is_transpose=True,
+                        start=(slot == 0), stop=(slot == SLOTS - 1),
+                    )
+            inverse = soft.tile([P, HD], F32)
+            nc.vector.reciprocal(out=inverse[:], in_=sums[:, 0, :])
+            pooled = soft.tile([P, HD], F32)
+            nc.vector.tensor_tensor(out=pooled[:], in0=sums[:, 1, :], in1=inverse[:], op=ALU.mult)
+            nc.sync.dma_start(out=pooled_chunks[c], in_=pooled[:])
+
+            k_rot = soft.tile([P, HD], F32)
+            nc.scalar.copy(out=k_rot[:, 0:NOPE], in_=pooled[:, 0:NOPE])
+            pairs = pooled[:, NOPE:HD].rearrange("p (j e) -> p j e", e=2)
+            turned = k_rot[:, NOPE:HD].rearrange("p (j e) -> p j e", e=2)
+            crossed = soft.tile([P, HALF, 2], F32)
+            nc.vector.tensor_tensor(
+                out=turned, in0=pairs, in1=sin_cos[:, 1, c, :].unsqueeze(2).to_broadcast([P, HALF, 2]), op=ALU.mult
+            )
+            nc.vector.tensor_tensor(out=crossed[:, :, 0], in0=pairs[:, :, 1], in1=neg_sin[:, c, :], op=ALU.mult)
+            nc.vector.tensor_tensor(out=crossed[:, :, 1], in0=pairs[:, :, 0], in1=sin_cos[:, 0, c, :], op=ALU.mult)
+            nc.vector.tensor_tensor(out=turned, in0=turned, in1=crossed[:], op=ALU.add)
+            nc.sync.dma_start(out=k_rot_chunks[c], in_=k_rot[:])
+
+        w_gate = quantise_weight(wgate_raw, nc.vector.tensor_copy)
+        x = [quantise_chunk(x_raw[0]), quantise_chunk(x_raw[1])]
+        w_kv = quantise_weight(wkv_raw, nc.scalar.copy)
+        for c in (1, 2, 3, 0):
+            before = (c - 1) % CHUNKS
+            gate = (project(w_gate, LO, x[before], "gate_lo"), project(w_gate, HI, x[c], "gate_hi"))
+            kv = (project(w_kv, LO, x[before], "kv_lo"), project(w_kv, HI, x[c], "kv_hi"))
+            if len(x) < CHUNKS:
+                x.append(quantise_chunk(x_raw[len(x)]))
+            pool_windows(c, gate, kv)

@@ -38,11 +38,12 @@ def tile_deepseekv4attention_pa_kernel(tc, hidden, wkv, wgate, ape, out_0, out_1
         const = ctx.enter_context(tc.tile_pool(name="const", bufs=1))
         weights = ctx.enter_context(tc.tile_pool(name="weights", bufs=2))
         tokens = ctx.enter_context(tc.tile_pool(name="tokens", bufs=CHUNKS))
-        stage_in = ctx.enter_context(tc.tile_pool(name="stage_in", bufs=3))
+        stage_in = ctx.enter_context(tc.tile_pool(name="stage_in", bufs=4))
         soft = ctx.enter_context(tc.tile_pool(name="soft", bufs=2))
-        psum_flip = ctx.enter_context(tc.psum_pool(name="psum_flip", bufs=3))
+        psum_flip = ctx.enter_context(tc.psum_pool(name="psum_flip", bufs=2))
         psum_mx = ctx.enter_context(tc.psum_pool(name="psum_mx", bufs=1))
         psum_sum = ctx.enter_context(tc.psum_pool(name="psum_sum", bufs=1))
+        ctx.enter_context(tc.manual_schedule())
 
         def load_weight(w):
             raw = weights.tile([P, PASSES, PACK, 2 * HD], BF16, name="w_raw")
@@ -62,8 +63,9 @@ def tile_deepseekv4attention_pa_kernel(tc, hidden, wkv, wgate, ape, out_0, out_1
         ape_rows = const.tile([P, P], BF16)
         nc.vector.memset(ape_rows[:], 0.0)
         nc.scalar.dma_start(out=ape_rows[0:SLOTS, :], in_=ape.rearrange("r (h f) -> (r h) f", h=2))
+        x_raw = [load_chunk(0)]
         wgate_raw = load_weight(wgate)
-        x_raw = [load_chunk(0), load_chunk(1)]
+        x_raw.append(load_chunk(1))
         wkv_raw = load_weight(wkv)
         x_raw.extend([load_chunk(2), load_chunk(3)])
 
@@ -92,14 +94,16 @@ def tile_deepseekv4attention_pa_kernel(tc, hidden, wkv, wgate, ape, out_0, out_1
         sin_cos = const.tile([P, 2, CHUNKS, HALF], F32)
         nc.scalar.activation(out=sin_cos[:], in_=phase[:], func=ACT.Sin, scale=2.0 * math.pi)
         neg_sin = const.tile([P, CHUNKS, HALF], F32)
-        nc.vector.tensor_single_scalar(out=neg_sin[:], in_=sin_cos[:, 0], scalar=-1.0, op=ALU.mult)
+        nc.scalar.activation(out=neg_sin[:], in_=phase[:, 0], func=ACT.Sin, scale=-2.0 * math.pi)
 
-        ape_rows_f32 = const.tile([P, P], F32)
-        nc.vector.tensor_copy(out=ape_rows_f32[:], in_=ape_rows[:])
-        ape_flip = psum_flip.tile([P, PASSES * 2, P], F32, tag="flip")
-        nc.tensor.transpose(ape_flip[:, 0, :], ape_rows_f32[:], ident[:])
         ape_col = const.tile([P, SLOTS], F32)
-        nc.vector.tensor_copy(out=ape_col[:], in_=ape_flip[:, 0, 0:SLOTS])
+
+        def spread_ape():
+            ape_rows_f32 = const.tile([P, P], F32)
+            nc.vector.tensor_copy(out=ape_rows_f32[:], in_=ape_rows[:])
+            ape_flip = psum_flip.tile([P, PASSES * 2, P], F32, tag="flip")
+            nc.tensor.transpose(ape_flip[:, 0, :], ape_rows_f32[:], ident[:])
+            nc.vector.tensor_copy(out=ape_col[:], in_=ape_flip[:, 0, 0:SLOTS])
 
         def offset(r, half):
             return ape_col[:, 2 * r + half : 2 * r + half + 1]
@@ -120,10 +124,9 @@ def tile_deepseekv4attention_pa_kernel(tc, hidden, wkv, wgate, ape, out_0, out_1
             )
             return codes, scales
 
-        def quantise_chunk(raw):
+        def flip_chunk(raw):
             words = raw[:].bitcast(F32)
-            codes = tokens.tile([P, PASSES, RATIO * P], U32, align_bytes=64, name="x_codes")
-            scales = tokens.tile([P, PASSES, RATIO * P], U8, align_bytes=64, name="x_scales")
+            grouped_pairs = []
             for pair in range(RATIO // 2):
                 grouped = stage_in.tile([P, PASSES, 2, P * PACK], BF16, align_bytes=64, name="x_grouped")
                 grouped_words = grouped[:].bitcast(F32)
@@ -136,6 +139,13 @@ def tile_deepseekv4attention_pa_kernel(tc, hidden, wkv, wgate, ape, out_0, out_1
                         out=grouped_words[:, :, r2, :].rearrange("p g (i u) -> p g i u", u=2),
                         in_=flip[:].rearrange("p (g u) i -> p g i u", u=2),
                     )
+                grouped_pairs.append(grouped)
+            return grouped_pairs
+
+        def quantise_chunk(grouped_pairs):
+            codes = tokens.tile([P, PASSES, RATIO * P], U32, align_bytes=64, name="x_codes")
+            scales = tokens.tile([P, PASSES, RATIO * P], U8, align_bytes=64, name="x_scales")
+            for pair, grouped in enumerate(grouped_pairs):
                 cols = slice(pair * 2 * P, (pair + 1) * 2 * P)
                 for g in range(PASSES):
                     nc.vector.quantize_mx(
@@ -162,60 +172,76 @@ def tile_deepseekv4attention_pa_kernel(tc, hidden, wkv, wgate, ape, out_0, out_1
                 )
             return product
 
-        def pool_windows(c, gate, kv):
-            shift = 1 if c == 0 else 0
-            source = (slice(0, P - shift), slice(0, P))
-            window = (slice(shift, P), slice(0, P))
-            slots = (slice(0, RATIO), slice(RATIO, SLOTS))
+        slots = (slice(0, RATIO), slice(RATIO, SLOTS))
 
+        def source(c, half):
+            return slice(0, P - 1) if c == 0 and half == LO else slice(0, P)
+
+        def window(c, half):
+            return slice(1, P) if c == 0 and half == LO else slice(0, P)
+
+        def width(c, half):
+            return P - 1 if c == 0 and half == LO else P
+
+        def largest_gate(c, gate):
             top = [soft.tile([P, P], F32, name="top_lo"), soft.tile([P, P], F32, name="top_hi")]
             for r in range(RATIO):
                 for half in (LO, HI):
                     if r == 0:
                         nc.vector.tensor_scalar(
-                            out=top[half][:, window[half]], in0=gate[half][:, r, source[half]],
+                            out=top[half][:, window(c, half)], in0=gate[half][:, r, source(c, half)],
                             scalar1=offset(r, half), scalar2=None, op0=ALU.add,
                         )
                     else:
                         nc.vector.scalar_tensor_tensor(
-                            out=top[half][:, window[half]], in0=gate[half][:, r, source[half]],
-                            scalar=offset(r, half), in1=top[half][:, window[half]], op0=ALU.add, op1=ALU.max,
+                            out=top[half][:, window(c, half)], in0=gate[half][:, r, source(c, half)],
+                            scalar=offset(r, half), in1=top[half][:, window(c, half)], op0=ALU.add, op1=ALU.max,
                         )
-            nc.vector.tensor_tensor(
-                out=top[HI][:, window[LO]], in0=top[HI][:, window[LO]], in1=top[LO][:, window[LO]], op=ALU.max
-            )
+            both = window(c, LO)
+            nc.vector.tensor_tensor(out=top[HI][:, both], in0=top[HI][:, both], in1=top[LO][:, both], op=ALU.max)
+            return top[HI]
 
+        def softmax_weights(c, gate, top):
             weight = soft.tile([P, SLOTS, P], F32)
-            weighted = soft.tile([P, SLOTS, P], F32)
-            if shift:
-                nc.vector.memset(weight[:, slots[LO], 0:shift], 0.0)
-                nc.vector.memset(weighted[:, slots[LO], 0:shift], 0.0)
+            if c == 0:
+                nc.vector.memset(weight[:, slots[LO], 0:1], 0.0)
             for half in (LO, HI):
-                width = P - shift if half == LO else P
+                windows = window(c, half)
                 nc.vector.tensor_tensor(
-                    out=weight[:, slots[half], window[half]], in0=gate[half][:, :, source[half]],
-                    in1=top[HI][:, window[half]].unsqueeze(1).to_broadcast([P, RATIO, width]), op=ALU.subtract,
+                    out=weight[:, slots[half], windows], in0=gate[half][:, :, source(c, half)],
+                    in1=top[:, windows].unsqueeze(1).to_broadcast([P, RATIO, width(c, half)]),
+                    op=ALU.subtract,
                 )
                 for r in range(RATIO):
-                    one = weight[:, half * RATIO + r, window[half]]
+                    one = weight[:, half * RATIO + r, windows]
                     nc.scalar.activation(out=one, in_=one, func=ACT.Exp, bias=offset(r, half), scale=1.0)
+            return weight
+
+        def multiply(c, weight, kv):
+            weighted = soft.tile([P, SLOTS, P], F32)
+            if c == 0:
+                nc.vector.memset(weighted[:, slots[LO], 0:1], 0.0)
             for half in (LO, HI):
                 nc.vector.tensor_tensor(
-                    out=weighted[:, slots[half], window[half]], in0=weight[:, slots[half], window[half]],
-                    in1=kv[half][:, :, source[half]], op=ALU.mult,
+                    out=weighted[:, slots[half], window(c, half)], in0=weight[:, slots[half], window(c, half)],
+                    in1=kv[half][:, :, source(c, half)], op=ALU.mult,
                 )
+            return weighted
 
-            sums = psum_sum.tile([P, 2, P], F32)
-            for which, terms in enumerate((weight, weighted)):
-                for slot in range(SLOTS):
-                    nc.tensor.matmul(
-                        out=sums[:, which, :], lhsT=terms[:, slot, :], rhs=ident[:], is_transpose=True,
-                        start=(slot == 0), stop=(slot == SLOTS - 1),
-                    )
+        def sum_slots(terms, tag):
+            total = psum_sum.tile([P, HD], F32, tag=tag)
+            for slot in range(SLOTS):
+                nc.tensor.matmul(
+                    out=total[:], lhsT=terms[:, slot, :], rhs=ident[:], is_transpose=True,
+                    start=(slot == 0), stop=(slot == SLOTS - 1),
+                )
+            return total
+
+        def finish(c, weight_sum, weighted_sum):
             inverse = soft.tile([P, HD], F32)
-            nc.vector.reciprocal(out=inverse[:], in_=sums[:, 0, :])
+            nc.vector.reciprocal(out=inverse[:], in_=weight_sum[:])
             pooled = soft.tile([P, HD], F32)
-            nc.vector.tensor_tensor(out=pooled[:], in0=sums[:, 1, :], in1=inverse[:], op=ALU.mult)
+            nc.vector.tensor_tensor(out=pooled[:], in0=weighted_sum[:], in1=inverse[:], op=ALU.mult)
             nc.sync.dma_start(out=pooled_chunks[c], in_=pooled[:])
 
             k_rot = soft.tile([P, HD], F32)
@@ -231,13 +257,38 @@ def tile_deepseekv4attention_pa_kernel(tc, hidden, wkv, wgate, ape, out_0, out_1
             nc.vector.tensor_tensor(out=turned, in0=turned, in1=crossed[:], op=ALU.add)
             nc.sync.dma_start(out=k_rot_chunks[c], in_=k_rot[:])
 
+        def project_halves(w, c, name):
+            return (project(w, LO, x[(c - 1) % CHUNKS], name + "_lo"), project(w, HI, x[c], name + "_hi"))
+
+        order = (1, 2, 3, 0)
+        grouped = [flip_chunk(x_raw[0])]
+        spread_ape()
         w_gate = quantise_weight(wgate_raw, nc.vector.tensor_copy)
-        x = [quantise_chunk(x_raw[0]), quantise_chunk(x_raw[1])]
-        w_kv = quantise_weight(wkv_raw, nc.scalar.copy)
-        for c in (1, 2, 3, 0):
-            before = (c - 1) % CHUNKS
-            gate = (project(w_gate, LO, x[before], "gate_lo"), project(w_gate, HI, x[c], "gate_hi"))
-            kv = (project(w_kv, LO, x[before], "kv_lo"), project(w_kv, HI, x[c], "kv_hi"))
+        x = [quantise_chunk(grouped[0])]
+        grouped.append(flip_chunk(x_raw[1]))
+        x.append(quantise_chunk(grouped[1]))
+        table_warmer = const.tile([P, 1], F32)
+        nc.scalar.activation(out=table_warmer[:], in_=position[:, 0:1], func=ACT.Exp, scale=0.0)
+        gate = project_halves(w_gate, order[0], "gate")
+        grouped.append(flip_chunk(x_raw[2]))
+        sums = None
+        for n, c in enumerate(order):
+            top = largest_gate(c, gate)
+            weight = softmax_weights(c, gate, top)
+            if n == 0:
+                w_kv = quantise_weight(wkv_raw, nc.vector.tensor_copy)
+                kv = project_halves(w_kv, c, "kv")
+            else:
+                finish(order[n - 1], sums[0], sums[1])
             if len(x) < CHUNKS:
-                x.append(quantise_chunk(x_raw[len(x)]))
-            pool_windows(c, gate, kv)
+                x.append(quantise_chunk(grouped[len(x)]))
+            if n + 1 < CHUNKS:
+                gate = project_halves(w_gate, order[n + 1], "gate")
+            weight_sum = sum_slots(weight, "weight_sum")
+            weighted = multiply(c, weight, kv)
+            sums = (weight_sum, sum_slots(weighted, "weighted_sum"))
+            if len(grouped) < CHUNKS:
+                grouped.append(flip_chunk(x_raw[len(grouped)]))
+            if n + 1 < CHUNKS:
+                kv = project_halves(w_kv, order[n + 1], "kv")
+        finish(order[CHUNKS - 1], sums[0], sums[1])

@@ -20,9 +20,12 @@ HALF = RD // 2
 NOPE = HD - RD
 PACK = 4
 PASSES = HID // (P * PACK)
-CHUNKS = S // RATIO // P
+WINDOWS = S // RATIO
+TILES = WINDOWS // P
 SLOTS = 2 * RATIO
 LO, HI = 0, 1
+FINE = 8
+BUNCH = 4
 ROUND = 1.5 * 2.0**23
 
 FLOPS = 2 * S * HID * 4 * HD
@@ -30,19 +33,18 @@ FLOPS = 2 * S * HID * 4 * HD
 
 def tile_deepseekv4attention_pa_kernel(tc, hidden, wkv, wgate, ape, out_0, out_1):
     nc = tc.nc
-    hidden_chunks = hidden.flatten_outer_dims().rearrange("(i c r) k -> c i (r k)", c=CHUNKS, r=RATIO)
-    k_rot_chunks = out_0.flatten_outer_dims().rearrange("(i c) f -> c i f", c=CHUNKS)
-    pooled_chunks = out_1.flatten_outer_dims().rearrange("(i c) f -> c i f", c=CHUNKS)
+    hidden_places = hidden.flatten_outer_dims().rearrange("(t i r) k -> r i t k", i=P, r=RATIO)
+    k_rot_rows = out_0.flatten_outer_dims().rearrange("(t i) f -> i t f", i=P)
+    pooled_rows = out_1.flatten_outer_dims().rearrange("(t i) f -> i t f", i=P)
 
     with ExitStack() as ctx:
         const = ctx.enter_context(tc.tile_pool(name="const", bufs=1))
         weights = ctx.enter_context(tc.tile_pool(name="weights", bufs=2))
-        tokens = ctx.enter_context(tc.tile_pool(name="tokens", bufs=CHUNKS))
+        tokens = ctx.enter_context(tc.tile_pool(name="tokens", bufs=RATIO))
         stage_in = ctx.enter_context(tc.tile_pool(name="stage_in", bufs=4))
-        soft = ctx.enter_context(tc.tile_pool(name="soft", bufs=2))
-        psum_flip = ctx.enter_context(tc.psum_pool(name="psum_flip", bufs=2))
-        psum_mx = ctx.enter_context(tc.psum_pool(name="psum_mx", bufs=1))
-        psum_sum = ctx.enter_context(tc.psum_pool(name="psum_sum", bufs=1))
+        soft = ctx.enter_context(tc.tile_pool(name="soft", bufs=1))
+        psum_two = ctx.enter_context(tc.psum_pool(name="psum_two", bufs=2))
+        psum_six = ctx.enter_context(tc.psum_pool(name="psum_six", bufs=6))
         ctx.enter_context(tc.manual_schedule())
 
         def load_weight(w):
@@ -53,47 +55,48 @@ def tile_deepseekv4attention_pa_kernel(tc, hidden, wkv, wgate, ape, out_0, out_1
             )
             return raw
 
-        def load_chunk(c):
-            raw = tokens.tile([P, RATIO * HID], BF16, name="x_raw")
-            for half in range(2):
-                cols = slice(half * 2 * HID, (half + 1) * 2 * HID)
-                nc.sync.dma_start(out=raw[:, cols], in_=hidden_chunks[c][:, cols])
+        def load_place(r):
+            raw = tokens.tile([P, TILES, HID], BF16, name="x_raw")
+            for pair in range(TILES // 2):
+                tiles = slice(2 * pair, 2 * pair + 2)
+                nc.sync.dma_start(out=raw[:, tiles, :], in_=hidden_places[r][:, tiles, :])
             return raw
 
         ape_rows = const.tile([P, P], BF16)
-        nc.vector.memset(ape_rows[:], 0.0)
+        nc.gpsimd.memset(ape_rows[:], 0.0)
         nc.scalar.dma_start(out=ape_rows[0:SLOTS, :], in_=ape.rearrange("r (h f) -> (r h) f", h=2))
-        x_raw = [load_chunk(0)]
         wgate_raw = load_weight(wgate)
-        x_raw.append(load_chunk(1))
         wkv_raw = load_weight(wkv)
-        x_raw.extend([load_chunk(2), load_chunk(3)])
+        x_raw = [load_place(r) for r in range(RATIO)]
 
+        position_int = const.tile([P, TILES], I32)
+        nc.gpsimd.iota(position_int[:], pattern=[[RATIO * P, TILES]], base=0, channel_multiplier=RATIO)
+        position = const.tile([P, TILES], F32)
+        nc.vector.tensor_copy(out=position[:], in_=position_int[:])
         ident = const.tile([P, P], F32)
         make_identity(nc, ident[:])
-
-        position_int = const.tile([P, CHUNKS], I32)
-        nc.gpsimd.iota(position_int[:], pattern=[[RATIO, CHUNKS]], base=0, channel_multiplier=RATIO * CHUNKS)
-        position = const.tile([P, CHUNKS], F32)
-        nc.vector.tensor_copy(out=position[:], in_=position_int[:])
-        turns = const.tile([P, CHUNKS, HALF], F32)
-        for j in range(HALF):
+        turns = const.tile([P, TILES, HALF], F32)
+        for j in range(FINE):
             nc.vector.tensor_single_scalar(
                 out=turns[:, :, j], in_=position[:], scalar=THETA ** (-j / HALF) / (2.0 * math.pi), op=ALU.mult
             )
-        whole_turns = const.tile([P, CHUNKS, HALF], F32)
+        for j in range(FINE, HALF, FINE):
+            nc.vector.tensor_single_scalar(
+                out=turns[:, :, j : j + FINE], in_=turns[:, :, 0:FINE], scalar=THETA ** (-j / HALF), op=ALU.mult
+            )
+        whole_turns = const.tile([P, TILES, HALF], F32)
         nc.vector.tensor_scalar(
             out=whole_turns[:], in0=turns[:], scalar1=ROUND, scalar2=ROUND, op0=ALU.add, op1=ALU.subtract
         )
-        phase = const.tile([P, 2, CHUNKS, HALF], F32)
+        phase = const.tile([P, 2, TILES, HALF], F32)
         nc.vector.tensor_tensor(out=phase[:, 0], in0=turns[:], in1=whole_turns[:], op=ALU.subtract)
         nc.vector.scalar_tensor_tensor(
             out=phase[:, 1], in0=phase[:, 0], scalar=-1.0, in1=phase[:, 0], op0=ALU.mult, op1=ALU.min
         )
         nc.vector.tensor_single_scalar(out=phase[:, 1], in_=phase[:, 1], scalar=0.25, op=ALU.add)
-        sin_cos = const.tile([P, 2, CHUNKS, HALF], F32)
+        sin_cos = const.tile([P, 2, TILES, HALF], F32)
         nc.scalar.activation(out=sin_cos[:], in_=phase[:], func=ACT.Sin, scale=2.0 * math.pi)
-        neg_sin = const.tile([P, CHUNKS, HALF], F32)
+        neg_sin = const.tile([P, TILES, HALF], F32)
         nc.scalar.activation(out=neg_sin[:], in_=phase[:, 0], func=ACT.Sin, scale=-2.0 * math.pi)
 
         ape_col = const.tile([P, SLOTS], F32)
@@ -101,17 +104,22 @@ def tile_deepseekv4attention_pa_kernel(tc, hidden, wkv, wgate, ape, out_0, out_1
         def spread_ape():
             ape_rows_f32 = const.tile([P, P], F32)
             nc.vector.tensor_copy(out=ape_rows_f32[:], in_=ape_rows[:])
-            ape_flip = psum_flip.tile([P, PASSES * 2, P], F32, tag="flip")
+            ape_flip = psum_two.tile([P, PASSES * 2, P], F32, tag="bank")
             nc.tensor.transpose(ape_flip[:, 0, :], ape_rows_f32[:], ident[:])
             nc.vector.tensor_copy(out=ape_col[:], in_=ape_flip[:, 0, 0:SLOTS])
 
         def offset(r, half):
             return ape_col[:, 2 * r + half : 2 * r + half + 1]
 
-        def quantise_weight(raw, copy):
+        weight = soft.tile([P, SLOTS, WINDOWS], F32)
+        weighted = soft.tile([P, SLOTS, WINDOWS], F32)
+        nc.vector.memset(weight[:, 0:RATIO, 0:1], 0.0)
+        nc.vector.memset(weighted[:, 0:RATIO, 0:1], 0.0)
+
+        def quantise_weight(raw):
             grouped = weights.tile([P, PASSES, 2 * HD, PACK], BF16, align_bytes=64, name="w_grouped")
             for g in range(PASSES):
-                copy(
+                nc.vector.tensor_copy(
                     out=grouped[:, g].rearrange("p (c i) t -> p c t i", i=4),
                     in_=raw[:, g].rearrange("p t (c i) -> p c t i", i=4),
                 )
@@ -124,45 +132,34 @@ def tile_deepseekv4attention_pa_kernel(tc, hidden, wkv, wgate, ape, out_0, out_1
             )
             return codes, scales
 
-        def flip_chunk(raw):
+        def quantise_tiles(raw, pair, codes, scales):
             words = raw[:].bitcast(F32)
-            grouped_pairs = []
-            for pair in range(RATIO // 2):
-                grouped = stage_in.tile([P, PASSES, 2, P * PACK], BF16, align_bytes=64, name="x_grouped")
-                grouped_words = grouped[:].bitcast(F32)
-                for r2 in range(2):
-                    first = (2 * pair + r2) * PASSES * 2
-                    flip = psum_flip.tile([P, PASSES * 2, P], F32, tag="flip")
-                    for q in range(PASSES * 2):
-                        nc.tensor.transpose(flip[:, q, :], words[:, (first + q) * P : (first + q + 1) * P], ident[:])
-                    nc.scalar.copy(
-                        out=grouped_words[:, :, r2, :].rearrange("p g (i u) -> p g i u", u=2),
-                        in_=flip[:].rearrange("p (g u) i -> p g i u", u=2),
-                    )
-                grouped_pairs.append(grouped)
-            return grouped_pairs
+            grouped = stage_in.tile([P, PASSES, 2, P * PACK], BF16, align_bytes=64, name="x_grouped")
+            grouped_words = grouped[:].bitcast(F32)
+            for t2 in range(2):
+                flip = psum_two.tile([P, PASSES * 2, P], F32, tag="bank")
+                for q in range(PASSES * 2):
+                    nc.tensor.transpose(flip[:, q, :], words[:, 2 * pair + t2, q * P : (q + 1) * P], ident[:])
+                nc.scalar.copy(
+                    out=grouped_words[:, :, t2, :].rearrange("p g (i u) -> p g i u", u=2),
+                    in_=flip[:].rearrange("p (g u) i -> p g i u", u=2),
+                )
+            cols = slice(pair * 2 * P, (pair + 1) * 2 * P)
+            for g in range(PASSES):
+                nc.vector.quantize_mx(
+                    out=codes[:, g, cols].bitcast(FP8X4),
+                    scales=scales[:, g, cols],
+                    in_=grouped[:, g].rearrange("p t x -> p (t x)"),
+                )
 
-        def quantise_chunk(grouped_pairs):
-            codes = tokens.tile([P, PASSES, RATIO * P], U32, align_bytes=64, name="x_codes")
-            scales = tokens.tile([P, PASSES, RATIO * P], U8, align_bytes=64, name="x_scales")
-            for pair, grouped in enumerate(grouped_pairs):
-                cols = slice(pair * 2 * P, (pair + 1) * 2 * P)
-                for g in range(PASSES):
-                    nc.vector.quantize_mx(
-                        out=codes[:, g, cols].bitcast(FP8X4),
-                        scales=scales[:, g, cols],
-                        in_=grouped[:, g].rearrange("p r x -> p (r x)"),
-                    )
-            return codes, scales
-
-        def project(w, half, x, tag):
+        def project(w, half, x, banks):
             w_codes, w_scales = w
             x_codes, x_scales = x
             features = slice(half * HD, (half + 1) * HD)
-            product = psum_mx.tile([P, RATIO, P], F32, tag=tag)
+            product = banks.tile([P, WINDOWS], F32, tag="bank")
             for g in range(PASSES):
                 nc.tensor.matmul_mx(
-                    out=product[:].rearrange("p r i -> p (r i)"),
+                    out=product[:],
                     lhsT=w_codes[:, g, features].bitcast(FP8X4),
                     lhsT_scale=w_scales[:, g, features],
                     rhs=x_codes[:, g, :].bitcast(FP8X4),
@@ -172,123 +169,110 @@ def tile_deepseekv4attention_pa_kernel(tc, hidden, wkv, wgate, ape, out_0, out_1
                 )
             return product
 
-        slots = (slice(0, RATIO), slice(RATIO, SLOTS))
+        w_gate = quantise_weight(wgate_raw)
+        w_kv = quantise_weight(wkv_raw)
+        largest = [soft.tile([P, WINDOWS], F32, name="largest_lo"), soft.tile([P, WINDOWS], F32, name="largest_hi")]
+        x = []
+        gate = []
 
-        def source(c, half):
-            return slice(0, P - 1) if c == 0 and half == LO else slice(0, P)
-
-        def window(c, half):
-            return slice(1, P) if c == 0 and half == LO else slice(0, P)
-
-        def width(c, half):
-            return P - 1 if c == 0 and half == LO else P
-
-        def largest_gate(c, gate):
-            top = [soft.tile([P, P], F32, name="top_lo"), soft.tile([P, P], F32, name="top_hi")]
-            for r in range(RATIO):
-                for half in (LO, HI):
-                    if r == 0:
-                        nc.vector.tensor_scalar(
-                            out=top[half][:, window(c, half)], in0=gate[half][:, r, source(c, half)],
-                            scalar1=offset(r, half), scalar2=None, op0=ALU.add,
-                        )
-                    else:
-                        nc.vector.scalar_tensor_tensor(
-                            out=top[half][:, window(c, half)], in0=gate[half][:, r, source(c, half)],
-                            scalar=offset(r, half), in1=top[half][:, window(c, half)], op0=ALU.add, op1=ALU.max,
-                        )
-            both = window(c, LO)
-            nc.vector.tensor_tensor(out=top[HI][:, both], in0=top[HI][:, both], in1=top[LO][:, both], op=ALU.max)
-            return top[HI]
-
-        def softmax_weights(c, gate, top):
-            weight = soft.tile([P, SLOTS, P], F32)
-            if c == 0:
-                nc.vector.memset(weight[:, slots[LO], 0:1], 0.0)
+        def gates_of_place(r, banks):
+            gate.append([project(w_gate, half, x[r], banks) for half in (LO, HI)])
             for half in (LO, HI):
-                windows = window(c, half)
-                nc.vector.tensor_tensor(
-                    out=weight[:, slots[half], windows], in0=gate[half][:, :, source(c, half)],
-                    in1=top[:, windows].unsqueeze(1).to_broadcast([P, RATIO, width(c, half)]),
-                    op=ALU.subtract,
-                )
-                for r in range(RATIO):
-                    one = weight[:, half * RATIO + r, windows]
-                    nc.scalar.activation(out=one, in_=one, func=ACT.Exp, bias=offset(r, half), scale=1.0)
-            return weight
+                if r == 0:
+                    nc.vector.tensor_scalar(
+                        out=largest[half][:], in0=gate[r][half][:], scalar1=offset(r, half), scalar2=None, op0=ALU.add
+                    )
+                else:
+                    nc.vector.scalar_tensor_tensor(
+                        out=largest[half][:], in0=gate[r][half][:], scalar=offset(r, half), in1=largest[half][:],
+                        op0=ALU.add, op1=ALU.max,
+                    )
 
-        def multiply(c, weight, kv):
-            weighted = soft.tile([P, SLOTS, P], F32)
-            if c == 0:
-                nc.vector.memset(weighted[:, slots[LO], 0:1], 0.0)
-            for half in (LO, HI):
-                nc.vector.tensor_tensor(
-                    out=weighted[:, slots[half], window(c, half)], in0=weight[:, slots[half], window(c, half)],
-                    in1=kv[half][:, :, source(c, half)], op=ALU.mult,
-                )
-            return weighted
-
-        def sum_slots(terms, tag):
-            total = psum_sum.tile([P, HD], F32, tag=tag)
-            for slot in range(SLOTS):
-                nc.tensor.matmul(
-                    out=total[:], lhsT=terms[:, slot, :], rhs=ident[:], is_transpose=True,
-                    start=(slot == 0), stop=(slot == SLOTS - 1),
-                )
-            return total
-
-        def finish(c, weight_sum, weighted_sum):
-            inverse = soft.tile([P, HD], F32)
-            nc.vector.reciprocal(out=inverse[:], in_=weight_sum[:])
-            pooled = soft.tile([P, HD], F32)
-            nc.vector.tensor_tensor(out=pooled[:], in0=weighted_sum[:], in1=inverse[:], op=ALU.mult)
-            nc.sync.dma_start(out=pooled_chunks[c], in_=pooled[:])
-
-            k_rot = soft.tile([P, HD], F32)
-            nc.scalar.copy(out=k_rot[:, 0:NOPE], in_=pooled[:, 0:NOPE])
-            pairs = pooled[:, NOPE:HD].rearrange("p (j e) -> p j e", e=2)
-            turned = k_rot[:, NOPE:HD].rearrange("p (j e) -> p j e", e=2)
-            crossed = soft.tile([P, HALF, 2], F32)
-            nc.vector.tensor_tensor(
-                out=turned, in0=pairs, in1=sin_cos[:, 1, c, :].unsqueeze(2).to_broadcast([P, HALF, 2]), op=ALU.mult
-            )
-            nc.vector.tensor_tensor(out=crossed[:, :, 0], in0=pairs[:, :, 1], in1=neg_sin[:, c, :], op=ALU.mult)
-            nc.vector.tensor_tensor(out=crossed[:, :, 1], in0=pairs[:, :, 0], in1=sin_cos[:, 0, c, :], op=ALU.mult)
-            nc.vector.tensor_tensor(out=turned, in0=turned, in1=crossed[:], op=ALU.add)
-            nc.sync.dma_start(out=k_rot_chunks[c], in_=k_rot[:])
-
-        def project_halves(w, c, name):
-            return (project(w, LO, x[(c - 1) % CHUNKS], name + "_lo"), project(w, HI, x[c], name + "_hi"))
-
-        order = (1, 2, 3, 0)
-        grouped = [flip_chunk(x_raw[0])]
-        spread_ape()
-        w_gate = quantise_weight(wgate_raw, nc.vector.tensor_copy)
-        x = [quantise_chunk(grouped[0])]
-        grouped.append(flip_chunk(x_raw[1]))
-        x.append(quantise_chunk(grouped[1]))
+        for r in range(RATIO):
+            codes = tokens.tile([P, PASSES, WINDOWS], U32, align_bytes=64, name="x_codes")
+            scales = tokens.tile([P, PASSES, WINDOWS], U8, align_bytes=64, name="x_scales")
+            x.append((codes, scales))
+            quantise_tiles(x_raw[r], 0, codes, scales)
+            if r > 0:
+                gates_of_place(r - 1, psum_six)
+            else:
+                spread_ape()
+            quantise_tiles(x_raw[r], 1, codes, scales)
         table_warmer = const.tile([P, 1], F32)
         nc.scalar.activation(out=table_warmer[:], in_=position[:, 0:1], func=ACT.Exp, scale=0.0)
-        gate = project_halves(w_gate, order[0], "gate")
-        grouped.append(flip_chunk(x_raw[2]))
-        sums = None
-        for n, c in enumerate(order):
-            top = largest_gate(c, gate)
-            weight = softmax_weights(c, gate, top)
-            if n == 0:
-                w_kv = quantise_weight(wkv_raw, nc.vector.tensor_copy)
-                kv = project_halves(w_kv, c, "kv")
-            else:
-                finish(order[n - 1], sums[0], sums[1])
-            if len(x) < CHUNKS:
-                x.append(quantise_chunk(grouped[len(x)]))
-            if n + 1 < CHUNKS:
-                gate = project_halves(w_gate, order[n + 1], "gate")
-            weight_sum = sum_slots(weight, "weight_sum")
-            weighted = multiply(c, weight, kv)
-            sums = (weight_sum, sum_slots(weighted, "weighted_sum"))
-            if len(grouped) < CHUNKS:
-                grouped.append(flip_chunk(x_raw[len(grouped)]))
-            if n + 1 < CHUNKS:
-                kv = project_halves(w_kv, order[n + 1], "kv")
-        finish(order[CHUNKS - 1], sums[0], sums[1])
+        gates_of_place(RATIO - 1, psum_two)
+        top = largest[HI]
+        nc.vector.tensor_tensor(
+            out=top[:, 1:WINDOWS], in0=top[:, 1:WINDOWS], in1=largest[LO][:, 0 : WINDOWS - 1], op=ALU.max
+        )
+
+        steps = [(r, half) for r in (3, 0, 1, 2) for half in (LO, HI)]
+
+        def source(half):
+            return slice(0, WINDOWS - 1) if half == LO else slice(0, WINDOWS)
+
+        def window(half):
+            return slice(1, WINDOWS) if half == LO else slice(0, WINDOWS)
+
+        def add_slots(total, terms, first_step):
+            for step in range(first_step, first_step + BUNCH):
+                r, half = steps[step]
+                for t in range(TILES):
+                    nc.tensor.matmul(
+                        out=total[:, t, :], lhsT=terms[:, half * RATIO + r, t * P : (t + 1) * P], rhs=ident[:],
+                        is_transpose=True, start=(step == 0 and t == 0), stop=(step == SLOTS - 1 and t == TILES - 1),
+                    )
+
+        def kv_of_step(step, banks):
+            r, half = steps[step]
+            return project(w_kv, half, x[r], banks)
+
+        kv = []
+        weight_sum = psum_six.tile([P, TILES, HD], F32, tag="bank")
+        weighted_sum = psum_six.tile([P, TILES, HD], F32, tag="bank")
+        for step, (r, half) in enumerate(steps):
+            one = weight[:, half * RATIO + r, window(half)]
+            nc.vector.scalar_tensor_tensor(
+                out=one, in0=gate[r][half][:, source(half)], scalar=offset(r, half), in1=top[:, window(half)],
+                op0=ALU.add, op1=ALU.subtract,
+            )
+            nc.scalar.activation(out=one, in_=one, func=ACT.Exp)
+            if step < 2:
+                kv.append(kv_of_step(len(kv), psum_two))
+            if step >= 4:
+                kv.append(kv_of_step(len(kv), psum_six))
+            if step % BUNCH == BUNCH - 1:
+                add_slots(weight_sum, weight, step - (BUNCH - 1))
+
+        log_sum = soft.tile([P, TILES, HD], F32)
+        nc.scalar.activation(out=log_sum[:], in_=weight_sum[:], func=ACT.Ln)
+        inverse = soft.tile([P, TILES, HD], F32)
+        nc.scalar.activation(out=inverse[:], in_=log_sum[:], func=ACT.Exp, scale=-1.0)
+
+        for step, (r, half) in enumerate(steps):
+            slot = half * RATIO + r
+            nc.vector.tensor_tensor(
+                out=weighted[:, slot, window(half)], in0=weight[:, slot, window(half)],
+                in1=kv[step][:, source(half)], op=ALU.mult,
+            )
+            if step < 2:
+                kv.append(kv_of_step(len(kv), psum_two))
+            if step % BUNCH == BUNCH - 1:
+                add_slots(weighted_sum, weighted, step - (BUNCH - 1))
+
+        pooled = soft.tile([P, TILES, HD], F32)
+        nc.vector.tensor_tensor(out=pooled[:], in0=weighted_sum[:], in1=inverse[:], op=ALU.mult)
+        nc.sync.dma_start(out=pooled_rows, in_=pooled[:])
+
+        k_rot = soft.tile([P, TILES, HD], F32)
+        nc.scalar.copy(out=k_rot[:, :, 0:NOPE], in_=pooled[:, :, 0:NOPE])
+        pairs = pooled[:, :, NOPE:HD].rearrange("p t (j e) -> p t j e", e=2)
+        turned = k_rot[:, :, NOPE:HD].rearrange("p t (j e) -> p t j e", e=2)
+        crossed = soft.tile([P, TILES, HALF, 2], F32)
+        nc.vector.tensor_tensor(
+            out=turned, in0=pairs, in1=sin_cos[:, 1].unsqueeze(3).to_broadcast([P, TILES, HALF, 2]), op=ALU.mult
+        )
+        nc.vector.tensor_tensor(out=crossed[:, :, :, 0], in0=pairs[:, :, :, 1], in1=neg_sin[:], op=ALU.mult)
+        nc.vector.tensor_tensor(out=crossed[:, :, :, 1], in0=pairs[:, :, :, 0], in1=sin_cos[:, 0], op=ALU.mult)
+        nc.vector.tensor_tensor(out=turned, in0=turned, in1=crossed[:], op=ALU.add)
+        nc.sync.dma_start(out=k_rot_rows, in_=k_rot[:])

@@ -25,7 +25,6 @@ TILES = WINDOWS // P
 SLOTS = 2 * RATIO
 LO, HI = 0, 1
 FINE = 8
-BUNCH = 4
 ROUND = 1.5 * 2.0**23
 
 FLOPS = 2 * S * HID * 4 * HD
@@ -65,9 +64,11 @@ def tile_deepseekv4attention_pa_kernel(tc, hidden, wkv, wgate, ape, out_0, out_1
         ape_rows = const.tile([P, P], BF16)
         nc.gpsimd.memset(ape_rows[:], 0.0)
         nc.scalar.dma_start(out=ape_rows[0:SLOTS, :], in_=ape.rearrange("r (h f) -> (r h) f", h=2))
+        x_raw = [load_place(0)]
         wgate_raw = load_weight(wgate)
+        x_raw.append(load_place(1))
         wkv_raw = load_weight(wkv)
-        x_raw = [load_place(r) for r in range(RATIO)]
+        x_raw.extend([load_place(2), load_place(3)])
 
         position_int = const.tile([P, TILES], I32)
         nc.gpsimd.iota(position_int[:], pattern=[[RATIO * P, TILES]], base=0, channel_multiplier=RATIO)
@@ -169,38 +170,39 @@ def tile_deepseekv4attention_pa_kernel(tc, hidden, wkv, wgate, ape, out_0, out_1
                 )
             return product
 
-        w_gate = quantise_weight(wgate_raw)
-        w_kv = quantise_weight(wkv_raw)
         largest = [soft.tile([P, WINDOWS], F32, name="largest_lo"), soft.tile([P, WINDOWS], F32, name="largest_hi")]
         x = []
-        gate = []
+        gate = [[], [], [], []]
 
-        def gates_of_place(r, banks):
-            gate.append([project(w_gate, half, x[r], banks) for half in (LO, HI)])
-            for half in (LO, HI):
-                if r == 0:
-                    nc.vector.tensor_scalar(
-                        out=largest[half][:], in0=gate[r][half][:], scalar1=offset(r, half), scalar2=None, op0=ALU.add
-                    )
-                else:
-                    nc.vector.scalar_tensor_tensor(
-                        out=largest[half][:], in0=gate[r][half][:], scalar=offset(r, half), in1=largest[half][:],
-                        op0=ALU.add, op1=ALU.max,
-                    )
+        def gates_of_place(r, half, banks):
+            gate[r].append(project(w_gate, half, x[r], banks))
+            if r == 0:
+                nc.vector.tensor_scalar(
+                    out=largest[half][:], in0=gate[r][half][:], scalar1=offset(r, half), scalar2=None, op0=ALU.add
+                )
+            else:
+                nc.vector.scalar_tensor_tensor(
+                    out=largest[half][:], in0=gate[r][half][:], scalar=offset(r, half), in1=largest[half][:],
+                    op0=ALU.add, op1=ALU.max,
+                )
 
         for r in range(RATIO):
             codes = tokens.tile([P, PASSES, WINDOWS], U32, align_bytes=64, name="x_codes")
             scales = tokens.tile([P, PASSES, WINDOWS], U8, align_bytes=64, name="x_scales")
             x.append((codes, scales))
-            quantise_tiles(x_raw[r], 0, codes, scales)
-            if r > 0:
-                gates_of_place(r - 1, psum_six)
-            else:
-                spread_ape()
-            quantise_tiles(x_raw[r], 1, codes, scales)
+            for pair, half in enumerate((LO, HI)):
+                quantise_tiles(x_raw[r], pair, codes, scales)
+                if r > 0:
+                    gates_of_place(r - 1, half, psum_six)
+                elif pair == 0:
+                    spread_ape()
+                    w_gate = quantise_weight(wgate_raw)
+            if r == 1:
+                w_kv = quantise_weight(wkv_raw)
         table_warmer = const.tile([P, 1], F32)
         nc.scalar.activation(out=table_warmer[:], in_=position[:, 0:1], func=ACT.Exp, scale=0.0)
-        gates_of_place(RATIO - 1, psum_two)
+        for half in (LO, HI):
+            gates_of_place(RATIO - 1, half, psum_two)
         top = largest[HI]
         nc.vector.tensor_tensor(
             out=top[:, 1:WINDOWS], in0=top[:, 1:WINDOWS], in1=largest[LO][:, 0 : WINDOWS - 1], op=ALU.max
@@ -214,51 +216,41 @@ def tile_deepseekv4attention_pa_kernel(tc, hidden, wkv, wgate, ape, out_0, out_1
         def window(half):
             return slice(1, WINDOWS) if half == LO else slice(0, WINDOWS)
 
-        def add_slots(total, terms, first_step):
-            for step in range(first_step, first_step + BUNCH):
-                r, half = steps[step]
-                for t in range(TILES):
-                    nc.tensor.matmul(
-                        out=total[:, t, :], lhsT=terms[:, half * RATIO + r, t * P : (t + 1) * P], rhs=ident[:],
-                        is_transpose=True, start=(step == 0 and t == 0), stop=(step == SLOTS - 1 and t == TILES - 1),
-                    )
-
-        def kv_of_step(step, banks):
+        def add_slot(total, terms, step):
             r, half = steps[step]
-            return project(w_kv, half, x[r], banks)
+            for t in range(TILES):
+                nc.tensor.matmul(
+                    out=total[:, t, :], lhsT=terms[:, half * RATIO + r, t * P : (t + 1) * P], rhs=ident[:],
+                    is_transpose=True, start=(step == 0 and t == 0), stop=(step == SLOTS - 1 and t == TILES - 1),
+                )
 
-        kv = []
-        weight_sum = psum_six.tile([P, TILES, HD], F32, tag="bank")
-        weighted_sum = psum_six.tile([P, TILES, HD], F32, tag="bank")
-        for step, (r, half) in enumerate(steps):
+        for r, half in steps:
             one = weight[:, half * RATIO + r, window(half)]
             nc.vector.scalar_tensor_tensor(
                 out=one, in0=gate[r][half][:, source(half)], scalar=offset(r, half), in1=top[:, window(half)],
                 op0=ALU.add, op1=ALU.subtract,
             )
             nc.scalar.activation(out=one, in_=one, func=ACT.Exp)
-            if step < 2:
-                kv.append(kv_of_step(len(kv), psum_two))
-            if step >= 4:
-                kv.append(kv_of_step(len(kv), psum_six))
-            if step % BUNCH == BUNCH - 1:
-                add_slots(weight_sum, weight, step - (BUNCH - 1))
 
+        weight_sum = psum_six.tile([P, TILES, HD], F32, tag="bank")
+        weighted_sum = psum_six.tile([P, TILES, HD], F32, tag="bank")
         log_sum = soft.tile([P, TILES, HD], F32)
-        nc.scalar.activation(out=log_sum[:], in_=weight_sum[:], func=ACT.Ln)
         inverse = soft.tile([P, TILES, HD], F32)
-        nc.scalar.activation(out=inverse[:], in_=log_sum[:], func=ACT.Exp, scale=-1.0)
-
         for step, (r, half) in enumerate(steps):
+            kv = project(w_kv, half, x[r], psum_six if 2 <= step < 6 else psum_two)
             slot = half * RATIO + r
             nc.vector.tensor_tensor(
                 out=weighted[:, slot, window(half)], in0=weight[:, slot, window(half)],
-                in1=kv[step][:, source(half)], op=ALU.mult,
+                in1=kv[:, source(half)], op=ALU.mult,
             )
-            if step < 2:
-                kv.append(kv_of_step(len(kv), psum_two))
-            if step % BUNCH == BUNCH - 1:
-                add_slots(weighted_sum, weighted, step - (BUNCH - 1))
+            for item in (2 * step, 2 * step + 1):
+                if item < SLOTS:
+                    add_slot(weight_sum, weight, item)
+                else:
+                    add_slot(weighted_sum, weighted, item - SLOTS)
+            if 2 * step + 2 == SLOTS:
+                nc.scalar.activation(out=log_sum[:], in_=weight_sum[:], func=ACT.Ln)
+                nc.scalar.activation(out=inverse[:], in_=log_sum[:], func=ACT.Exp, scale=-1.0)
 
         pooled = soft.tile([P, TILES, HD], F32)
         nc.vector.tensor_tensor(out=pooled[:], in0=weighted_sum[:], in1=inverse[:], op=ALU.mult)

@@ -42,8 +42,7 @@ def tile_deepseekv4attention_pa_kernel(tc, hidden, wkv, wgate, ape, out_0, out_1
         tokens = ctx.enter_context(tc.tile_pool(name="tokens", bufs=RATIO))
         stage_in = ctx.enter_context(tc.tile_pool(name="stage_in", bufs=4))
         soft = ctx.enter_context(tc.tile_pool(name="soft", bufs=1))
-        psum_two = ctx.enter_context(tc.psum_pool(name="psum_two", bufs=2))
-        psum_six = ctx.enter_context(tc.psum_pool(name="psum_six", bufs=6))
+        psum = ctx.enter_context(tc.psum_pool(name="psum", bufs=8))
         ctx.enter_context(tc.manual_schedule())
 
         def load_weight(w):
@@ -66,9 +65,8 @@ def tile_deepseekv4attention_pa_kernel(tc, hidden, wkv, wgate, ape, out_0, out_1
         nc.scalar.dma_start(out=ape_rows[0:SLOTS, :], in_=ape.rearrange("r (h f) -> (r h) f", h=2))
         x_raw = [load_place(0)]
         wgate_raw = load_weight(wgate)
-        x_raw.append(load_place(1))
+        x_raw.extend([load_place(1), load_place(2), load_place(3)])
         wkv_raw = load_weight(wkv)
-        x_raw.extend([load_place(2), load_place(3)])
 
         position_int = const.tile([P, TILES], I32)
         nc.gpsimd.iota(position_int[:], pattern=[[RATIO * P, TILES]], base=0, channel_multiplier=RATIO)
@@ -105,7 +103,7 @@ def tile_deepseekv4attention_pa_kernel(tc, hidden, wkv, wgate, ape, out_0, out_1
         def spread_ape():
             ape_rows_f32 = const.tile([P, P], F32)
             nc.vector.tensor_copy(out=ape_rows_f32[:], in_=ape_rows[:])
-            ape_flip = psum_two.tile([P, PASSES * 2, P], F32, tag="bank")
+            ape_flip = psum.tile([P, PASSES * 2, P], F32, tag="bank")
             nc.tensor.transpose(ape_flip[:, 0, :], ape_rows_f32[:], ident[:])
             nc.vector.tensor_copy(out=ape_col[:], in_=ape_flip[:, 0, 0:SLOTS])
 
@@ -117,13 +115,16 @@ def tile_deepseekv4attention_pa_kernel(tc, hidden, wkv, wgate, ape, out_0, out_1
         nc.vector.memset(weight[:, 0:RATIO, 0:1], 0.0)
         nc.vector.memset(weighted[:, 0:RATIO, 0:1], 0.0)
 
-        def quantise_weight(raw):
+        def regroup_weight(raw, copy):
             grouped = weights.tile([P, PASSES, 2 * HD, PACK], BF16, align_bytes=64, name="w_grouped")
             for g in range(PASSES):
-                nc.vector.tensor_copy(
+                copy(
                     out=grouped[:, g].rearrange("p (c i) t -> p c t i", i=4),
                     in_=raw[:, g].rearrange("p t (c i) -> p c t i", i=4),
                 )
+            return grouped
+
+        def quantise_weight(grouped):
             codes = weights.tile([P, PASSES, 2 * HD], U32, align_bytes=64, name="w_codes")
             scales = weights.tile([P, PASSES, 2 * HD], U8, align_bytes=64, name="w_scales")
             nc.vector.quantize_mx(
@@ -138,7 +139,7 @@ def tile_deepseekv4attention_pa_kernel(tc, hidden, wkv, wgate, ape, out_0, out_1
             grouped = stage_in.tile([P, PASSES, 2, P * PACK], BF16, align_bytes=64, name="x_grouped")
             grouped_words = grouped[:].bitcast(F32)
             for t2 in range(2):
-                flip = psum_two.tile([P, PASSES * 2, P], F32, tag="bank")
+                flip = psum.tile([P, PASSES * 2, P], F32, tag="bank")
                 for q in range(PASSES * 2):
                     nc.tensor.transpose(flip[:, q, :], words[:, 2 * pair + t2, q * P : (q + 1) * P], ident[:])
                 nc.scalar.copy(
@@ -153,11 +154,11 @@ def tile_deepseekv4attention_pa_kernel(tc, hidden, wkv, wgate, ape, out_0, out_1
                     in_=grouped[:, g].rearrange("p t x -> p (t x)"),
                 )
 
-        def project(w, half, x, banks):
+        def project(w, half, x):
             w_codes, w_scales = w
             x_codes, x_scales = x
             features = slice(half * HD, (half + 1) * HD)
-            product = banks.tile([P, WINDOWS], F32, tag="bank")
+            product = psum.tile([P, WINDOWS], F32, tag="bank")
             for g in range(PASSES):
                 nc.tensor.matmul_mx(
                     out=product[:],
@@ -174,8 +175,8 @@ def tile_deepseekv4attention_pa_kernel(tc, hidden, wkv, wgate, ape, out_0, out_1
         x = []
         gate = [[], [], [], []]
 
-        def gates_of_place(r, half, banks):
-            gate[r].append(project(w_gate, half, x[r], banks))
+        def gates_of_place(r, half):
+            gate[r].append(project(w_gate, half, x[r]))
             if r == 0:
                 nc.vector.tensor_scalar(
                     out=largest[half][:], in0=gate[r][half][:], scalar1=offset(r, half), scalar2=None, op0=ALU.add
@@ -186,29 +187,29 @@ def tile_deepseekv4attention_pa_kernel(tc, hidden, wkv, wgate, ape, out_0, out_1
                     op0=ALU.add, op1=ALU.max,
                 )
 
-        for r in range(RATIO):
-            codes = tokens.tile([P, PASSES, WINDOWS], U32, align_bytes=64, name="x_codes")
-            scales = tokens.tile([P, PASSES, WINDOWS], U8, align_bytes=64, name="x_scales")
-            x.append((codes, scales))
-            for pair, half in enumerate((LO, HI)):
-                quantise_tiles(x_raw[r], pair, codes, scales)
-                if r > 0:
-                    gates_of_place(r - 1, half, psum_six)
-                elif pair == 0:
-                    spread_ape()
-                    w_gate = quantise_weight(wgate_raw)
-            if r == 1:
-                w_kv = quantise_weight(wkv_raw)
-        table_warmer = const.tile([P, 1], F32)
-        nc.scalar.activation(out=table_warmer[:], in_=position[:, 0:1], func=ACT.Exp, scale=0.0)
-        for half in (LO, HI):
-            gates_of_place(RATIO - 1, half, psum_two)
+        for r in range(RATIO + 1):
+            if r < RATIO:
+                codes = tokens.tile([P, PASSES, WINDOWS], U32, align_bytes=64, name="x_codes")
+                scales = tokens.tile([P, PASSES, WINDOWS], U8, align_bytes=64, name="x_scales")
+                x.append((codes, scales))
+                for pair in range(TILES // 2):
+                    quantise_tiles(x_raw[r], pair, codes, scales)
+            else:
+                wkv_grouped = regroup_weight(wkv_raw, nc.scalar.copy)
+                table_warmer = const.tile([P, 1], F32)
+                nc.scalar.activation(out=table_warmer[:], in_=position[:, 0:1], func=ACT.Exp, scale=0.0)
+            if r == 0:
+                spread_ape()
+                w_gate = quantise_weight(regroup_weight(wgate_raw, nc.vector.tensor_copy))
+            else:
+                for half in (LO, HI):
+                    gates_of_place(r - 1, half)
         top = largest[HI]
         nc.vector.tensor_tensor(
             out=top[:, 1:WINDOWS], in0=top[:, 1:WINDOWS], in1=largest[LO][:, 0 : WINDOWS - 1], op=ALU.max
         )
 
-        steps = [(r, half) for r in (3, 0, 1, 2) for half in (LO, HI)]
+        steps = [(r, half) for r in range(RATIO) for half in (LO, HI)]
 
         def source(half):
             return slice(0, WINDOWS - 1) if half == LO else slice(0, WINDOWS)
@@ -224,31 +225,34 @@ def tile_deepseekv4attention_pa_kernel(tc, hidden, wkv, wgate, ape, out_0, out_1
                     is_transpose=True, start=(step == 0 and t == 0), stop=(step == SLOTS - 1 and t == TILES - 1),
                 )
 
-        for r, half in steps:
+        for step, (r, half) in enumerate(steps):
             one = weight[:, half * RATIO + r, window(half)]
             nc.vector.scalar_tensor_tensor(
                 out=one, in0=gate[r][half][:, source(half)], scalar=offset(r, half), in1=top[:, window(half)],
                 op0=ALU.add, op1=ALU.subtract,
             )
             nc.scalar.activation(out=one, in_=one, func=ACT.Exp)
+            if step == 0:
+                w_kv = quantise_weight(wkv_grouped)
 
-        weight_sum = psum_six.tile([P, TILES, HD], F32, tag="bank")
-        weighted_sum = psum_six.tile([P, TILES, HD], F32, tag="bank")
+        weight_sum = psum.tile([P, TILES, HD], F32, tag="bank")
+        weighted_sum = psum.tile([P, TILES, HD], F32, tag="bank")
         log_sum = soft.tile([P, TILES, HD], F32)
         inverse = soft.tile([P, TILES, HD], F32)
-        for step, (r, half) in enumerate(steps):
-            kv = project(w_kv, half, x[r], psum_six if 2 <= step < 6 else psum_two)
-            slot = half * RATIO + r
-            nc.vector.tensor_tensor(
-                out=weighted[:, slot, window(half)], in0=weight[:, slot, window(half)],
-                in1=kv[:, source(half)], op=ALU.mult,
-            )
-            for item in (2 * step, 2 * step + 1):
+        for r in range(RATIO):
+            for half in (LO, HI):
+                kv = project(w_kv, half, x[r])
+                slot = half * RATIO + r
+                nc.vector.tensor_tensor(
+                    out=weighted[:, slot, window(half)], in0=weight[:, slot, window(half)],
+                    in1=kv[:, source(half)], op=ALU.mult,
+                )
+            for item in range(4 * r, 4 * r + 4):
                 if item < SLOTS:
                     add_slot(weight_sum, weight, item)
                 else:
                     add_slot(weighted_sum, weighted, item - SLOTS)
-            if 2 * step + 2 == SLOTS:
+            if 4 * r + 4 == SLOTS:
                 nc.scalar.activation(out=log_sum[:], in_=weight_sum[:], func=ACT.Ln)
                 nc.scalar.activation(out=inverse[:], in_=log_sum[:], func=ACT.Exp, scale=-1.0)
 

@@ -55,9 +55,8 @@ def tile_deepseekv4attention_pa_kernel(tc, hidden, wkv, wgate, ape, out_0, out_1
 
         def load_place(r):
             raw = tokens.tile([P, TILES, HID], BF16, name="x_raw")
-            for pair in range(TILES // 2):
-                tiles = slice(2 * pair, 2 * pair + 2)
-                nc.sync.dma_start(out=raw[:, tiles, :], in_=hidden_places[r][:, tiles, :])
+            for t in range(TILES):
+                nc.sync.dma_start(out=raw[:, t, :], in_=hidden_places[r][:, t, :])
             return raw
 
         ape_rows = const.tile([P, P], BF16)
@@ -65,8 +64,9 @@ def tile_deepseekv4attention_pa_kernel(tc, hidden, wkv, wgate, ape, out_0, out_1
         nc.scalar.dma_start(out=ape_rows[0:SLOTS, :], in_=ape.rearrange("r (h f) -> (r h) f", h=2))
         x_raw = [load_place(0)]
         wgate_raw = load_weight(wgate)
-        x_raw.extend([load_place(1), load_place(2), load_place(3)])
+        x_raw.append(load_place(1))
         wkv_raw = load_weight(wkv)
+        x_raw.extend([load_place(2), load_place(3)])
 
         position_int = const.tile([P, TILES], I32)
         nc.gpsimd.iota(position_int[:], pattern=[[RATIO * P, TILES]], base=0, channel_multiplier=RATIO)
@@ -171,21 +171,28 @@ def tile_deepseekv4attention_pa_kernel(tc, hidden, wkv, wgate, ape, out_0, out_1
                 )
             return product
 
-        largest = [soft.tile([P, WINDOWS], F32, name="largest_lo"), soft.tile([P, WINDOWS], F32, name="largest_hi")]
+        top = soft.tile([P, WINDOWS], F32)
         x = []
-        gate = [[], [], [], []]
+        gate = {}
 
-        def gates_of_place(r, half):
-            gate[r].append(project(w_gate, half, x[r]))
-            if r == 0:
-                nc.vector.tensor_scalar(
-                    out=largest[half][:], in0=gate[r][half][:], scalar1=offset(r, half), scalar2=None, op0=ALU.add
-                )
-            else:
-                nc.vector.scalar_tensor_tensor(
-                    out=largest[half][:], in0=gate[r][half][:], scalar=offset(r, half), in1=largest[half][:],
-                    op0=ALU.add, op1=ALU.max,
-                )
+        def source(half):
+            return slice(0, WINDOWS - 1) if half == LO else slice(0, WINDOWS)
+
+        def window(half):
+            return slice(1, WINDOWS) if half == LO else slice(0, WINDOWS)
+
+        def gates_of_place(r):
+            for half in (HI, LO):
+                gate[(r, half)] = project(w_gate, half, x[r])
+                if r == 0 and half == HI:
+                    nc.vector.tensor_scalar(
+                        out=top[:], in0=gate[(r, half)][:], scalar1=offset(r, half), scalar2=None, op0=ALU.add
+                    )
+                else:
+                    nc.vector.scalar_tensor_tensor(
+                        out=top[:, window(half)], in0=gate[(r, half)][:, source(half)], scalar=offset(r, half),
+                        in1=top[:, window(half)], op0=ALU.add, op1=ALU.max,
+                    )
 
         for r in range(RATIO + 1):
             if r < RATIO:
@@ -195,27 +202,17 @@ def tile_deepseekv4attention_pa_kernel(tc, hidden, wkv, wgate, ape, out_0, out_1
                 for pair in range(TILES // 2):
                     quantise_tiles(x_raw[r], pair, codes, scales)
             else:
-                wkv_grouped = regroup_weight(wkv_raw, nc.scalar.copy)
                 table_warmer = const.tile([P, 1], F32)
                 nc.scalar.activation(out=table_warmer[:], in_=position[:, 0:1], func=ACT.Exp, scale=0.0)
             if r == 0:
                 spread_ape()
                 w_gate = quantise_weight(regroup_weight(wgate_raw, nc.vector.tensor_copy))
             else:
-                for half in (LO, HI):
-                    gates_of_place(r - 1, half)
-        top = largest[HI]
-        nc.vector.tensor_tensor(
-            out=top[:, 1:WINDOWS], in0=top[:, 1:WINDOWS], in1=largest[LO][:, 0 : WINDOWS - 1], op=ALU.max
-        )
+                gates_of_place(r - 1)
+            if r == 1:
+                w_kv = quantise_weight(regroup_weight(wkv_raw, nc.vector.tensor_copy))
 
         steps = [(r, half) for r in range(RATIO) for half in (LO, HI)]
-
-        def source(half):
-            return slice(0, WINDOWS - 1) if half == LO else slice(0, WINDOWS)
-
-        def window(half):
-            return slice(1, WINDOWS) if half == LO else slice(0, WINDOWS)
 
         def add_slot(total, terms, step):
             r, half = steps[step]
@@ -225,21 +222,18 @@ def tile_deepseekv4attention_pa_kernel(tc, hidden, wkv, wgate, ape, out_0, out_1
                     is_transpose=True, start=(step == 0 and t == 0), stop=(step == SLOTS - 1 and t == TILES - 1),
                 )
 
-        for step, (r, half) in enumerate(steps):
+        for r, half in steps:
             one = weight[:, half * RATIO + r, window(half)]
             nc.vector.scalar_tensor_tensor(
-                out=one, in0=gate[r][half][:, source(half)], scalar=offset(r, half), in1=top[:, window(half)],
+                out=one, in0=gate[(r, half)][:, source(half)], scalar=offset(r, half), in1=top[:, window(half)],
                 op0=ALU.add, op1=ALU.subtract,
             )
             nc.scalar.activation(out=one, in_=one, func=ACT.Exp)
-            if step == 0:
-                w_kv = quantise_weight(wkv_grouped)
 
         weight_sum = psum.tile([P, TILES, HD], F32, tag="bank")
         weighted_sum = psum.tile([P, TILES, HD], F32, tag="bank")
-        log_sum = soft.tile([P, TILES, HD], F32)
-        inverse = soft.tile([P, TILES, HD], F32)
-        for r in range(RATIO):
+
+        def multiply_place(r):
             for half in (LO, HI):
                 kv = project(w_kv, half, x[r])
                 slot = half * RATIO + r
@@ -247,14 +241,22 @@ def tile_deepseekv4attention_pa_kernel(tc, hidden, wkv, wgate, ape, out_0, out_1
                     out=weighted[:, slot, window(half)], in0=weight[:, slot, window(half)],
                     in1=kv[:, source(half)], op=ALU.mult,
                 )
-            for item in range(4 * r, 4 * r + 4):
-                if item < SLOTS:
-                    add_slot(weight_sum, weight, item)
-                else:
-                    add_slot(weighted_sum, weighted, item - SLOTS)
-            if 4 * r + 4 == SLOTS:
-                nc.scalar.activation(out=log_sum[:], in_=weight_sum[:], func=ACT.Ln)
-                nc.scalar.activation(out=inverse[:], in_=log_sum[:], func=ACT.Exp, scale=-1.0)
+
+        def add_places(first_place):
+            for total, terms in ((weight_sum, weight), (weighted_sum, weighted)):
+                for step in range(2 * first_place, 2 * first_place + 4):
+                    add_slot(total, terms, step)
+
+        for r in range(RATIO - 1):
+            multiply_place(r)
+        add_places(0)
+        multiply_place(RATIO - 1)
+        add_places(2)
+
+        root = soft.tile([P, TILES, HD], F32)
+        nc.scalar.activation(out=root[:], in_=weight_sum[:], func=ACT.Abs_reciprocal_sqrt)
+        inverse = soft.tile([P, TILES, HD], F32)
+        nc.scalar.activation(out=inverse[:], in_=root[:], func=ACT.Square)
 
         pooled = soft.tile([P, TILES, HD], F32)
         nc.vector.tensor_tensor(out=pooled[:], in0=weighted_sum[:], in1=inverse[:], op=ALU.mult)

@@ -112,6 +112,7 @@ def tile_deepseekv4attention_pa_kernel(tc, hidden, wkv, wgate, ape, out_0, out_1
 
         weight = soft.tile([P, SLOTS, WINDOWS], F32)
         weighted = soft.tile([P, SLOTS, WINDOWS], F32)
+        weight_pair = soft.tile([P, RATIO, WINDOWS], F32)
         nc.vector.memset(weight[:, 0:RATIO, 0:1], 0.0)
         nc.vector.memset(weighted[:, 0:RATIO, 0:1], 0.0)
 
@@ -214,14 +215,6 @@ def tile_deepseekv4attention_pa_kernel(tc, hidden, wkv, wgate, ape, out_0, out_1
 
         steps = [(r, half) for r in range(RATIO) for half in (LO, HI)]
 
-        def add_slot(total, terms, step):
-            r, half = steps[step]
-            for t in range(TILES):
-                nc.tensor.matmul(
-                    out=total[:, t, :], lhsT=terms[:, half * RATIO + r, t * P : (t + 1) * P], rhs=ident[:],
-                    is_transpose=True, start=(step == 0 and t == 0), stop=(step == SLOTS - 1 and t == TILES - 1),
-                )
-
         for r, half in steps:
             one = weight[:, half * RATIO + r, window(half)]
             nc.vector.scalar_tensor_tensor(
@@ -229,6 +222,10 @@ def tile_deepseekv4attention_pa_kernel(tc, hidden, wkv, wgate, ape, out_0, out_1
                 op0=ALU.add, op1=ALU.subtract,
             )
             nc.scalar.activation(out=one, in_=one, func=ACT.Exp)
+            if half == HI:
+                nc.gpsimd.tensor_tensor(
+                    out=weight_pair[:, r, :], in0=weight[:, r, :], in1=weight[:, RATIO + r, :], op=ALU.add
+                )
 
         weight_sum = psum.tile([P, TILES, HD], F32, tag="bank")
         weighted_sum = psum.tile([P, TILES, HD], F32, tag="bank")
@@ -242,16 +239,30 @@ def tile_deepseekv4attention_pa_kernel(tc, hidden, wkv, wgate, ape, out_0, out_1
                     in1=kv[:, source(half)], op=ALU.mult,
                 )
 
-        def add_places(first_place):
-            for total, terms in ((weight_sum, weight), (weighted_sum, weighted)):
-                for step in range(2 * first_place, 2 * first_place + 4):
-                    add_slot(total, terms, step)
+        def add_up(total, terms, first, last):
+            for t in range(TILES):
+                nc.tensor.matmul(
+                    out=total[:, t, :], lhsT=terms[:, t * P : (t + 1) * P], rhs=ident[:], is_transpose=True,
+                    start=(first and t == 0), stop=(last and t == TILES - 1),
+                )
+
+        def add_weights(r):
+            add_up(weight_sum, weight_pair[:, r, :], r == 0, r == RATIO - 1)
+
+        def add_weighted(r):
+            for half in (LO, HI):
+                add_up(weighted_sum, weighted[:, half * RATIO + r, :], r == 0 and half == LO, r == RATIO - 1 and half == HI)
 
         for r in range(RATIO - 1):
             multiply_place(r)
-        add_places(0)
+        add_weights(0)
+        add_weights(1)
+        add_weighted(0)
         multiply_place(RATIO - 1)
-        add_places(2)
+        add_weights(2)
+        add_weights(3)
+        for r in range(1, RATIO):
+            add_weighted(r)
 
         root = soft.tile([P, TILES, HD], F32)
         nc.scalar.activation(out=root[:], in_=weight_sum[:], func=ACT.Abs_reciprocal_sqrt)

import math
from contextlib import ExitStack

import concourse.mybir as mybir
from concourse.masks import make_identity

F32 = mybir.dt.float32
BF16 = mybir.dt.bfloat16
I32 = mybir.dt.int32
U32 = mybir.dt.uint32
U8 = mybir.dt.uint8
FP8X4 = mybir.dt.float8_e4m3fn_x4
ALU = mybir.AluOpType
ACT = mybir.ActivationFunctionType

P = 128
S, HID, HD, RD, RATIO = 2048, 1024, 128, 64, 4
THETA = 10000.0
HALF = RD // 2
NOPE = HD - RD
PACK = 4
PASSES = HID // (P * PACK)
WINDOWS = S // RATIO
TILES = WINDOWS // P
SLOTS = 2 * RATIO
LO, HI = 0, 1
FINE = 8
ROUND = 1.5 * 2.0**23

FLOPS = 2 * S * HID * 4 * HD


def tile_deepseekv4attention_pa_kernel(tc, hidden, wkv, wgate, ape, out_0, out_1):
    nc = tc.nc
    hidden_places = hidden.flatten_outer_dims().rearrange("(t i r) k -> r i t k", i=P, r=RATIO)
    k_rot_rows = out_0.flatten_outer_dims().rearrange("(t i) f -> i t f", i=P)
    pooled_rows = out_1.flatten_outer_dims().rearrange("(t i) f -> i t f", i=P)

    with ExitStack() as ctx:
        const = ctx.enter_context(tc.tile_pool(name="const", bufs=1))
        weights = ctx.enter_context(tc.tile_pool(name="weights", bufs=2))
        tokens = ctx.enter_context(tc.tile_pool(name="tokens", bufs=RATIO))
        stage_in = ctx.enter_context(tc.tile_pool(name="stage_in", bufs=4))
        soft = ctx.enter_context(tc.tile_pool(name="soft", bufs=1))
        psum = ctx.enter_context(tc.psum_pool(name="psum", bufs=8))
        ctx.enter_context(tc.manual_schedule())

        def load_weight(w):
            raw = weights.tile([P, PASSES, PACK, 2 * HD], BF16, name="w_raw")
            nc.sync.dma_start(
                out=raw[:].rearrange("p g (u e) c -> p (g u) (e c)", e=2),
                in_=w.rearrange("(gu p e) c -> p gu (e c)", p=P, e=2),
            )
            return raw

        def load_place(r):
            raw = tokens.tile([P, TILES, HID], BF16, name="x_raw")
            for t in range(TILES):
                nc.sync.dma_start(out=raw[:, t, :], in_=hidden_places[r][:, t, :])
            return raw

        ape_rows = const.tile([P, P], BF16)
        nc.gpsimd.memset(ape_rows[:], 0.0)
        nc.scalar.dma_start(out=ape_rows[0:SLOTS, :], in_=ape.rearrange("r (h f) -> (r h) f", h=2))
        x_raw = [load_place(0)]
        wgate_raw = load_weight(wgate)
        x_raw.append(load_place(1))
        wkv_raw = load_weight(wkv)
        x_raw.extend([load_place(2), load_place(3)])

        position_int = const.tile([P, TILES], I32)
        nc.gpsimd.iota(position_int[:], pattern=[[RATIO * P, TILES]], base=0, channel_multiplier=RATIO)
        position = const.tile([P, TILES], F32)
        nc.vector.tensor_copy(out=position[:], in_=position_int[:])
        ident = const.tile([P, P], F32)
        make_identity(nc, ident[:])
        turns = const.tile([P, TILES, HALF], F32)
        for j in range(FINE):
            nc.vector.tensor_single_scalar(
                out=turns[:, :, j], in_=position[:], scalar=THETA ** (-j / HALF) / (2.0 * math.pi), op=ALU.mult
            )
        for j in range(FINE, HALF, FINE):
            nc.vector.tensor_single_scalar(
                out=turns[:, :, j : j + FINE], in_=turns[:, :, 0:FINE], scalar=THETA ** (-j / HALF), op=ALU.mult
            )
        whole_turns = const.tile([P, TILES, HALF], F32)
        nc.vector.tensor_scalar(
            out=whole_turns[:], in0=turns[:], scalar1=ROUND, scalar2=ROUND, op0=ALU.add, op1=ALU.subtract
        )
        phase = const.tile([P, 2, TILES, HALF], F32)
        nc.vector.tensor_tensor(out=phase[:, 0], in0=turns[:], in1=whole_turns[:], op=ALU.subtract)
        nc.vector.scalar_tensor_tensor(
            out=phase[:, 1], in0=phase[:, 0], scalar=-1.0, in1=phase[:, 0], op0=ALU.mult, op1=ALU.min
        )
        nc.vector.tensor_single_scalar(out=phase[:, 1], in_=phase[:, 1], scalar=0.25, op=ALU.add)
        sin_cos = const.tile([P, 2, TILES, HALF], F32)
        nc.scalar.activation(out=sin_cos[:], in_=phase[:], func=ACT.Sin, scale=2.0 * math.pi)
        neg_sin = const.tile([P, TILES, HALF], F32)
        nc.scalar.activation(out=neg_sin[:], in_=phase[:, 0], func=ACT.Sin, scale=-2.0 * math.pi)

        ape_col = const.tile([P, SLOTS], F32)

        def spread_ape():
            ape_rows_f32 = const.tile([P, P], F32)
            nc.vector.tensor_copy(out=ape_rows_f32[:], in_=ape_rows[:])
            ape_flip = psum.tile([P, PASSES * 2, P], F32, tag="bank")
            nc.tensor.transpose(ape_flip[:, 0, :], ape_rows_f32[:], ident[:])
            nc.vector.tensor_copy(out=ape_col[:], in_=ape_flip[:, 0, 0:SLOTS])

        def offset(r, half):
            return ape_col[:, 2 * r + half : 2 * r + half + 1]

        weight = soft.tile([P, SLOTS, WINDOWS], F32)
        weighted = soft.tile([P, SLOTS, WINDOWS], F32)
        weight_pair = soft.tile([P, RATIO, WINDOWS], F32)
        nc.vector.memset(weight[:, 0:RATIO, 0:1], 0.0)
        nc.vector.memset(weighted[:, 0:RATIO, 0:1], 0.0)

        def regroup_weight(raw, copy):
            grouped = weights.tile([P, PASSES, 2 * HD, PACK], BF16, align_bytes=64, name="w_grouped")
            for g in range(PASSES):
                copy(
                    out=grouped[:, g].rearrange("p (c i) t -> p c t i", i=4),
                    in_=raw[:, g].rearrange("p t (c i) -> p c t i", i=4),
                )
            return grouped

        def quantise_weight(grouped):
            codes = weights.tile([P, PASSES, 2 * HD], U32, align_bytes=64, name="w_codes")
            scales = weights.tile([P, PASSES, 2 * HD], U8, align_bytes=64, name="w_scales")
            nc.vector.quantize_mx(
                out=codes[:].rearrange("p g c -> p (g c)").bitcast(FP8X4),
                scales=scales[:].rearrange("p g c -> p (g c)"),
                in_=grouped[:].rearrange("p g c t -> p (g c t)"),
            )
            return codes, scales

        def quantise_tiles(raw, pair, codes, scales):
            words = raw[:].bitcast(F32)
            grouped = stage_in.tile([P, PASSES, 2, P * PACK], BF16, align_bytes=64, name="x_grouped")
            grouped_words = grouped[:].bitcast(F32)
            for t2 in range(2):
                flip = psum.tile([P, PASSES * 2, P], F32, tag="bank")
                for q in range(PASSES * 2):
                    nc.tensor.transpose(flip[:, q, :], words[:, 2 * pair + t2, q * P : (q + 1) * P], ident[:])
                nc.scalar.copy(
                    out=grouped_words[:, :, t2, :].rearrange("p g (i u) -> p g i u", u=2),
                    in_=flip[:].rearrange("p (g u) i -> p g i u", u=2),
                )
            cols = slice(pair * 2 * P, (pair + 1) * 2 * P)
            for g in range(PASSES):
                nc.vector.quantize_mx(
                    out=codes[:, g, cols].bitcast(FP8X4),
                    scales=scales[:, g, cols],
                    in_=grouped[:, g].rearrange("p t x -> p (t x)"),
                )

        def project(w, half, x):
            w_codes, w_scales = w
            x_codes, x_scales = x
            features = slice(half * HD, (half + 1) * HD)
            product = psum.tile([P, WINDOWS], F32, tag="bank")
            for g in range(PASSES):
                nc.tensor.matmul_mx(
                    out=product[:],
                    lhsT=w_codes[:, g, features].bitcast(FP8X4),
                    lhsT_scale=w_scales[:, g, features],
                    rhs=x_codes[:, g, :].bitcast(FP8X4),
                    rhs_scale=x_scales[:, g, :],
                    start=(g == 0),
                    stop=(g == PASSES - 1),
                )
            return product

        top = soft.tile([P, WINDOWS], F32)
        x = []
        gate = {}

        def source(half):
            return slice(0, WINDOWS - 1) if half == LO else slice(0, WINDOWS)

        def window(half):
            return slice(1, WINDOWS) if half == LO else slice(0, WINDOWS)

        def gates_of_place(r):
            for half in (HI, LO):
                gate[(r, half)] = project(w_gate, half, x[r])
                if r == 0 and half == HI:
                    nc.vector.tensor_scalar(
                        out=top[:], in0=gate[(r, half)][:], scalar1=offset(r, half), scalar2=None, op0=ALU.add
                    )
                else:
                    nc.vector.scalar_tensor_tensor(
                        out=top[:, window(half)], in0=gate[(r, half)][:, source(half)], scalar=offset(r, half),
                        in1=top[:, window(half)], op0=ALU.add, op1=ALU.max,
                    )

        for r in range(RATIO + 1):
            if r < RATIO:
                codes = tokens.tile([P, PASSES, WINDOWS], U32, align_bytes=64, name="x_codes")
                scales = tokens.tile([P, PASSES, WINDOWS], U8, align_bytes=64, name="x_scales")
                x.append((codes, scales))
                for pair in range(TILES // 2):
                    quantise_tiles(x_raw[r], pair, codes, scales)
            else:
                table_warmer = const.tile([P, 1], F32)
                nc.scalar.activation(out=table_warmer[:], in_=position[:, 0:1], func=ACT.Exp, scale=0.0)
            if r == 0:
                spread_ape()
                w_gate = quantise_weight(regroup_weight(wgate_raw, nc.vector.tensor_copy))
            else:
                gates_of_place(r - 1)
            if r == 1:
                w_kv = quantise_weight(regroup_weight(wkv_raw, nc.vector.tensor_copy))

        steps = [(r, half) for r in range(RATIO) for half in (LO, HI)]

        for r, half in steps:
            one = weight[:, half * RATIO + r, window(half)]
            nc.vector.scalar_tensor_tensor(
                out=one, in0=gate[(r, half)][:, source(half)], scalar=offset(r, half), in1=top[:, window(half)],
                op0=ALU.add, op1=ALU.subtract,
            )
            nc.scalar.activation(out=one, in_=one, func=ACT.Exp)
            if half == HI:
                nc.gpsimd.tensor_tensor(
                    out=weight_pair[:, r, :], in0=weight[:, r, :], in1=weight[:, RATIO + r, :], op=ALU.add
                )

        weight_sum = psum.tile([P, TILES, HD], F32, tag="bank")
        weighted_sum = psum.tile([P, TILES, HD], F32, tag="bank")

        def multiply_place(r):
            for half in (LO, HI):
                kv = project(w_kv, half, x[r])
                slot = half * RATIO + r
                nc.vector.tensor_tensor(
                    out=weighted[:, slot, window(half)], in0=weight[:, slot, window(half)],
                    in1=kv[:, source(half)], op=ALU.mult,
                )

        def add_up(total, terms, first, last):
            for t in range(TILES):
                nc.tensor.matmul(
                    out=total[:, t, :], lhsT=terms[:, t * P : (t + 1) * P], rhs=ident[:], is_transpose=True,
                    start=(first and t == 0), stop=(last and t == TILES - 1),
                )

        def add_weights(r):
            add_up(weight_sum, weight_pair[:, r, :], r == 0, r == RATIO - 1)

        def add_weighted(r):
            for half in (LO, HI):
                add_up(weighted_sum, weighted[:, half * RATIO + r, :], r == 0 and half == LO, r == RATIO - 1 and half == HI)

        for r in range(RATIO - 1):
            multiply_place(r)
        add_weights(0)
        add_weights(1)
        add_weighted(0)
        multiply_place(RATIO - 1)
        add_weights(2)
        add_weights(3)
        for r in range(1, RATIO):
            add_weighted(r)

        root = soft.tile([P, TILES, HD], F32)
        nc.scalar.activation(out=root[:], in_=weight_sum[:], func=ACT.Abs_reciprocal_sqrt)
        inverse = soft.tile([P, TILES, HD], F32)
        nc.scalar.activation(out=inverse[:], in_=root[:], func=ACT.Square)

        pooled = soft.tile([P, TILES, HD], F32)
        nc.vector.tensor_tensor(out=pooled[:], in0=weighted_sum[:], in1=inverse[:], op=ALU.mult)
        nc.sync.dma_start(out=pooled_rows, in_=pooled[:])

        k_rot = soft.tile([P, TILES, HD], F32)
        nc.scalar.copy(out=k_rot[:, :, 0:NOPE], in_=pooled[:, :, 0:NOPE])
        pairs = pooled[:, :, NOPE:HD].rearrange("p t (j e) -> p t j e", e=2)
        turned = k_rot[:, :, NOPE:HD].rearrange("p t (j e) -> p t j e", e=2)
        crossed = soft.tile([P, TILES, HALF, 2], F32)
        nc.vector.tensor_tensor(
            out=turned, in0=pairs, in1=sin_cos[:, 1].unsqueeze(3).to_broadcast([P, TILES, HALF, 2]), op=ALU.mult
        )
        nc.vector.tensor_tensor(out=crossed[:, :, :, 0], in0=pairs[:, :, :, 1], in1=neg_sin[:], op=ALU.mult)
        nc.vector.tensor_tensor(out=crossed[:, :, :, 1], in0=pairs[:, :, :, 0], in1=sin_cos[:, 0], op=ALU.mult)
        nc.vector.tensor_tensor(out=turned, in0=turned, in1=crossed[:], op=ALU.add)
        nc.sync.dma_start(out=k_rot_rows, in_=k_rot[:])
